import numpy as np
import ml_dtypes

BF16 = ml_dtypes.bfloat16


def bf(x):
    return np.asarray(x, np.float32).astype(BF16)


def f32(x):
    return np.asarray(x, np.float32)


def f64(x):
    return np.asarray(x).astype(np.float64)


def striped(idx):
    return np.tile(idx.reshape(-1, 16).T, (8, 1))


D, C, CH, HH, NH, T, S, N = 256, 256, 128, 64, 2, 512, 4096, 1024


def setup_inputs():
    x = bf(np.random.standard_normal((D, N)))
    w = bf(np.random.standard_normal((D, C)) / np.sqrt(D))
    ang = np.random.uniform(0.0, 2.0 * np.pi, (HH, T + 1))
    ang = np.concatenate([ang[:, :T], ang[:, 1:]], axis=1)
    ang = np.tile(ang, (NH, 1))
    base = f32(np.random.standard_normal((C, S)))
    return {"x": x, "w": w, "cos_t": f32(np.cos(ang)), "sin_t": f32(np.sin(ang)), "base": base, "offs": striped(np.random.permutation(S)[:N])}


def reference(x, w, cos_t, sin_t, base, offs):
    idx = offs[:16].T.reshape(-1)
    k = f64(w).T @ f64(x)
    kr, ki = k[:CH], k[CH:]
    out = f64(base).copy()
    out[:CH, idx] = kr * f64(cos_t) + (-(ki * f64(sin_t)))
    out[CH:, idx] = kr * f64(sin_t) + ki * f64(cos_t)
    return out

@@ -1,0 +1,67 @@
+import concourse.mybir as mybir
+
+P = 128
+D = 256
+N = 1024
+S = 4096
+BANK = 512
+FLOPS = 2 * D * (2 * P) * N
+
+BF16, F32, U16 = mybir.dt.bfloat16, mybir.dt.float32, mybir.dt.uint16
+MULT, ADD = mybir.AluOpType.mult, mybir.AluOpType.add
+
+
+def tile_ebtattention_kernel(tc, x, w, cos_t, sin_t, base, offs, out):
+    nc = tc.nc
+    with tc.tile_pool(name="held", bufs=1) as held, tc.psum_pool(name="psum", bufs=1) as psum:
+        offsets = held.tile([P, N // 16], U16, name="offsets")
+        nc.sync.dma_start(offsets[:], offs)
+        w_sb = held.tile([P, D // P, 2 * P], BF16, name="w_sb")
+        nc.sync.dma_start(w_sb[:], w.rearrange("(kb p) m -> p kb m", p=P))
+        x_sb = held.tile([P, D // P, N], BF16, name="x_sb")
+        nc.sync.dma_start(x_sb[:], x.rearrange("(kb p) n -> p kb n", p=P))
+        cos_sb = held.tile([P, N], F32, name="cos_sb")
+        nc.scalar.dma_start(cos_sb[:], cos_t)
+        sin_sb = held.tile([P, N], F32, name="sin_sb")
+        nc.scalar.dma_start(sin_sb[:], sin_t)
+
+        windows = [held.tile([P, S], F32, name=f"window{h}") for h in range(2)]
+        for h in range(2):
+            rows = base[h * P : (h + 1) * P, :]
+            nc.sync.dma_start(windows[h][:, : S // 2], rows[:, : S // 2])
+            nc.scalar.dma_start(windows[h][:, S // 2 :], rows[:, S // 2 :])
+
+        neg_sin = held.tile([P, N], F32, name="neg_sin")
+        nc.scalar.mul(neg_sin[:], sin_sb[:], -1.0)
+
+        k_ps = [[psum.tile([P, BANK], F32, name=f"k_ps{h}{c}") for c in range(N // BANK)] for h in range(2)]
+        for c in range(N // BANK):
+            for h in range(2):
+                for kb in range(D // P):
+                    nc.tensor.matmul(
+                        k_ps[h][c][:],
+                        w_sb[:, kb, h * P : (h + 1) * P],
+                        x_sb[:, kb, c * BANK : (c + 1) * BANK],
+                        start=(kb == 0),
+                        stop=(kb == D // P - 1),
+                    )
+
+        kr_cos = held.tile([P, N], F32, name="kr_cos")
+        ki_neg_sin = held.tile([P, N], F32, name="ki_neg_sin")
+        kr_sin = held.tile([P, N], F32, name="kr_sin")
+        ki_cos = held.tile([P, N], F32, name="ki_cos")
+        for product, h, angle in (
+            (kr_cos, 0, cos_sb),
+            (ki_neg_sin, 1, neg_sin),
+            (kr_sin, 0, sin_sb),
+            (ki_cos, 1, cos_sb),
+        ):
+            for c in range(N // BANK):
+                cols = slice(c * BANK, (c + 1) * BANK)
+                nc.vector.tensor_tensor(product[:, cols], k_ps[h][c][:], angle[:, cols], MULT)
+
+        for h, (first, second) in enumerate(((kr_cos, ki_neg_sin), (kr_sin, ki_cos))):
+            nc.vector.tensor_tensor(windows[h][:].indirect(offsets[:]), first[:], second[:], ADD)
+            rows = out[h * P : (h + 1) * P, :]
+            nc.sync.dma_start(rows[:, : S // 2], windows[h][:, : S // 2])
+            nc.scalar.dma_start(rows[:, S // 2 :], windows[h][:, S // 2 :])

@@ -13,35 +13,33 @@ MULT, ADD = mybir.AluOpType.mult, mybir.AluOpType.add
 
 def tile_ebtattention_kernel(tc, x, w, cos_t, sin_t, base, offs, out):
     nc = tc.nc
+    chunks = [slice(c * BANK, (c + 1) * BANK) for c in range(N // BANK)]
     with tc.tile_pool(name="held", bufs=1) as held, tc.psum_pool(name="psum", bufs=1) as psum:
         offsets = held.tile([P, N // 16], U16, name="offsets")
-        nc.sync.dma_start(offsets[:], offs)
         w_sb = held.tile([P, D // P, 2 * P], BF16, name="w_sb")
-        nc.sync.dma_start(w_sb[:], w.rearrange("(kb p) m -> p kb m", p=P))
         x_sb = held.tile([P, D // P, N], BF16, name="x_sb")
-        nc.sync.dma_start(x_sb[:], x.rearrange("(kb p) n -> p kb n", p=P))
         cos_sb = held.tile([P, N], F32, name="cos_sb")
-        nc.scalar.dma_start(cos_sb[:], cos_t)
         sin_sb = held.tile([P, N], F32, name="sin_sb")
-        nc.scalar.dma_start(sin_sb[:], sin_t)
-
         windows = [held.tile([P, S], F32, name=f"window{h}") for h in range(2)]
-        for h in range(2):
-            rows = base[h * P : (h + 1) * P, :]
-            nc.sync.dma_start(windows[h][:, : S // 2], rows[:, : S // 2])
-            nc.scalar.dma_start(windows[h][:, S // 2 :], rows[:, S // 2 :])
+        x_blocks = x.rearrange("(kb p) n -> p kb n", p=P)
 
-        neg_sin = held.tile([P, N], F32, name="neg_sin")
-        nc.scalar.mul(neg_sin[:], sin_sb[:], -1.0)
+        nc.sync.dma_start(offsets[:], offs)
+        nc.sync.dma_start(w_sb[:], w.rearrange("(kb p) m -> p kb m", p=P))
+        for cols in chunks:
+            nc.sync.dma_start(x_sb[:, :, cols], x_blocks[:, :, cols])
+            nc.sync.dma_start(cos_sb[:, cols], cos_t[:, cols])
+            nc.sync.dma_start(sin_sb[:, cols], sin_t[:, cols])
+        for h in range(2):
+            nc.sync.dma_start(windows[h][:], base[h * P : (h + 1) * P, :])
 
         k_ps = [[psum.tile([P, BANK], F32, name=f"k_ps{h}{c}") for c in range(N // BANK)] for h in range(2)]
-        for c in range(N // BANK):
+        for c, cols in enumerate(chunks):
             for h in range(2):
                 for kb in range(D // P):
                     nc.tensor.matmul(
                         k_ps[h][c][:],
                         w_sb[:, kb, h * P : (h + 1) * P],
-                        x_sb[:, kb, c * BANK : (c + 1) * BANK],
+                        x_sb[:, kb, cols],
                         start=(kb == 0),
                         stop=(kb == D // P - 1),
                     )
@@ -50,15 +48,13 @@ def tile_ebtattention_kernel(tc, x, w, cos_t, sin_t, base, offs, out):
         ki_neg_sin = held.tile([P, N], F32, name="ki_neg_sin")
         kr_sin = held.tile([P, N], F32, name="kr_sin")
         ki_cos = held.tile([P, N], F32, name="ki_cos")
-        for product, h, angle in (
-            (kr_cos, 0, cos_sb),
-            (ki_neg_sin, 1, neg_sin),
-            (kr_sin, 0, sin_sb),
-            (ki_cos, 1, cos_sb),
-        ):
-            for c in range(N // BANK):
-                cols = slice(c * BANK, (c + 1) * BANK)
-                nc.vector.tensor_tensor(product[:, cols], k_ps[h][c][:], angle[:, cols], MULT)
+        neg_sin = held.tile([P, N], F32, name="neg_sin")
+        for c, cols in enumerate(chunks):
+            nc.scalar.mul(neg_sin[:, cols], sin_sb[:, cols], -1.0)
+            nc.vector.tensor_tensor(kr_cos[:, cols], k_ps[0][c][:], cos_sb[:, cols], MULT)
+            nc.vector.tensor_tensor(ki_neg_sin[:, cols], k_ps[1][c][:], neg_sin[:, cols], MULT)
+            nc.vector.tensor_tensor(kr_sin[:, cols], k_ps[0][c][:], sin_sb[:, cols], MULT)
+            nc.vector.tensor_tensor(ki_cos[:, cols], k_ps[1][c][:], cos_sb[:, cols], MULT)
 
         for h, (first, second) in enumerate(((kr_cos, ki_neg_sin), (kr_sin, ki_cos))):
             nc.vector.tensor_tensor(windows[h][:].indirect(offsets[:]), first[:], second[:], ADD)

@@ -23,14 +23,15 @@ def tile_ebtattention_kernel(tc, x, w, cos_t, sin_t, base, offs, out):
         windows = [held.tile([P, S], F32, name=f"window{h}") for h in range(2)]
         x_blocks = x.rearrange("(kb p) n -> p kb n", p=P)
 
-        nc.sync.dma_start(offsets[:], offs)
         nc.sync.dma_start(w_sb[:], w.rearrange("(kb p) m -> p kb m", p=P))
         for cols in chunks:
             nc.sync.dma_start(x_sb[:, :, cols], x_blocks[:, :, cols])
             nc.sync.dma_start(cos_sb[:, cols], cos_t[:, cols])
             nc.sync.dma_start(sin_sb[:, cols], sin_t[:, cols])
+        nc.sync.dma_start(offsets[:], offs)
         for h in range(2):
-            nc.sync.dma_start(windows[h][:], base[h * P : (h + 1) * P, :])
+            for slots in (slice(0, S // 2), slice(S // 2, S)):
+                nc.sync.dma_start(windows[h][:, slots], base[h * P : (h + 1) * P, slots])
 
         k_ps = [[psum.tile([P, BANK], F32, name=f"k_ps{h}{c}") for c in range(N // BANK)] for h in range(2)]
         for c, cols in enumerate(chunks):

@@ -25,7 +25,7 @@ def tile_ebtattention_kernel(tc, x, w, cos_t, sin_t, base, offs, out):
 
         nc.sync.dma_start(w_sb[:], w.rearrange("(kb p) m -> p kb m", p=P))
         for cols in chunks:
-            nc.sync.dma_start(x_sb[:, :, cols], x_blocks[:, :, cols])
+            nc.scalar.dma_start(x_sb[:, :, cols], x_blocks[:, :, cols])
             nc.sync.dma_start(cos_sb[:, cols], cos_t[:, cols])
             nc.sync.dma_start(sin_sb[:, cols], sin_t[:, cols])
         nc.sync.dma_start(offsets[:], offs)

@@ -18,8 +18,8 @@ def tile_ebtattention_kernel(tc, x, w, cos_t, sin_t, base, offs, out):
         offsets = held.tile([P, N // 16], U16, name="offsets")
         w_sb = held.tile([P, D // P, 2 * P], BF16, name="w_sb")
         x_sb = held.tile([P, D // P, N], BF16, name="x_sb")
-        cos_sb = held.tile([P, N], F32, name="cos_sb")
-        sin_sb = held.tile([P, N], F32, name="sin_sb")
+        trig = held.tile([P, 3, N], F32, name="trig")
+        neg_sin, cos_sb, sin_sb = (trig[:, plane, :] for plane in range(3))
         windows = [held.tile([P, S], F32, name=f"window{h}") for h in range(2)]
         x_blocks = x.rearrange("(kb p) n -> p kb n", p=P)
 
@@ -45,20 +45,16 @@ def tile_ebtattention_kernel(tc, x, w, cos_t, sin_t, base, offs, out):
                         stop=(kb == D // P - 1),
                     )
 
-        kr_cos = held.tile([P, N], F32, name="kr_cos")
-        ki_neg_sin = held.tile([P, N], F32, name="ki_neg_sin")
-        kr_sin = held.tile([P, N], F32, name="kr_sin")
-        ki_cos = held.tile([P, N], F32, name="ki_cos")
-        neg_sin = held.tile([P, N], F32, name="neg_sin")
+        kr_products = held.tile([P, 2, N], F32, name="kr_products")
+        ki_products = held.tile([P, 2, N], F32, name="ki_products")
         for c, cols in enumerate(chunks):
             nc.scalar.mul(neg_sin[:, cols], sin_sb[:, cols], -1.0)
-            nc.vector.tensor_tensor(kr_cos[:, cols], k_ps[0][c][:], cos_sb[:, cols], MULT)
-            nc.vector.tensor_tensor(ki_neg_sin[:, cols], k_ps[1][c][:], neg_sin[:, cols], MULT)
-            nc.vector.tensor_tensor(kr_sin[:, cols], k_ps[0][c][:], sin_sb[:, cols], MULT)
-            nc.vector.tensor_tensor(ki_cos[:, cols], k_ps[1][c][:], cos_sb[:, cols], MULT)
+            for half, (products, planes) in enumerate(((kr_products, slice(1, 3)), (ki_products, slice(0, 2)))):
+                k_twice = k_ps[half][c][:].unsqueeze(1).to_broadcast([P, 2, BANK])
+                nc.vector.tensor_tensor(products[:, :, cols], k_twice, trig[:, planes, cols], MULT)
 
-        for h, (first, second) in enumerate(((kr_cos, ki_neg_sin), (kr_sin, ki_cos))):
-            nc.vector.tensor_tensor(windows[h][:].indirect(offsets[:]), first[:], second[:], ADD)
+        for h in range(2):
+            nc.vector.tensor_tensor(windows[h][:].indirect(offsets[:]), kr_products[:, h, :], ki_products[:, h, :], ADD)
             rows = out[h * P : (h + 1) * P, :]
             nc.sync.dma_start(rows[:, : S // 2], windows[h][:, : S // 2])
             nc.scalar.dma_start(rows[:, S // 2 :], windows[h][:, S // 2 :])

import concourse.mybir as mybir

P = 128
D = 256
N = 1024
S = 4096
BANK = 512
FLOPS = 2 * D * (2 * P) * N

BF16, F32, U16 = mybir.dt.bfloat16, mybir.dt.float32, mybir.dt.uint16
MULT, ADD = mybir.AluOpType.mult, mybir.AluOpType.add


def tile_ebtattention_kernel(tc, x, w, cos_t, sin_t, base, offs, out):
    nc = tc.nc
    chunks = [slice(c * BANK, (c + 1) * BANK) for c in range(N // BANK)]
    with tc.tile_pool(name="held", bufs=1) as held, tc.psum_pool(name="psum", bufs=1) as psum:
        offsets = held.tile([P, N // 16], U16, name="offsets")
        w_sb = held.tile([P, D // P, 2 * P], BF16, name="w_sb")
        x_sb = held.tile([P, D // P, N], BF16, name="x_sb")
        trig = held.tile([P, 3, N], F32, name="trig")
        neg_sin, cos_sb, sin_sb = (trig[:, plane, :] for plane in range(3))
        windows = [held.tile([P, S], F32, name=f"window{h}") for h in range(2)]
        x_blocks = x.rearrange("(kb p) n -> p kb n", p=P)

        nc.sync.dma_start(w_sb[:], w.rearrange("(kb p) m -> p kb m", p=P))
        for cols in chunks:
            nc.scalar.dma_start(x_sb[:, :, cols], x_blocks[:, :, cols])
            nc.sync.dma_start(cos_sb[:, cols], cos_t[:, cols])
            nc.sync.dma_start(sin_sb[:, cols], sin_t[:, cols])
        nc.sync.dma_start(offsets[:], offs)
        for h in range(2):
            for slots in (slice(0, S // 2), slice(S // 2, S)):
                nc.sync.dma_start(windows[h][:, slots], base[h * P : (h + 1) * P, slots])

        k_ps = [[psum.tile([P, BANK], F32, name=f"k_ps{h}{c}") for c in range(N // BANK)] for h in range(2)]
        for c, cols in enumerate(chunks):
            for h in range(2):
                for kb in range(D // P):
                    nc.tensor.matmul(
                        k_ps[h][c][:],
                        w_sb[:, kb, h * P : (h + 1) * P],
                        x_sb[:, kb, cols],
                        start=(kb == 0),
                        stop=(kb == D // P - 1),
                    )

        kr_products = held.tile([P, 2, N], F32, name="kr_products")
        ki_products = held.tile([P, 2, N], F32, name="ki_products")
        for c, cols in enumerate(chunks):
            nc.scalar.mul(neg_sin[:, cols], sin_sb[:, cols], -1.0)
            for half, (products, planes) in enumerate(((kr_products, slice(1, 3)), (ki_products, slice(0, 2)))):
                k_twice = k_ps[half][c][:].unsqueeze(1).to_broadcast([P, 2, BANK])
                nc.vector.tensor_tensor(products[:, :, cols], k_twice, trig[:, planes, cols], MULT)

        for h in range(2):
            nc.vector.tensor_tensor(windows[h][:].indirect(offsets[:]), kr_products[:, h, :], ki_products[:, h, :], ADD)
            rows = out[h * P : (h + 1) * P, :]
            nc.sync.dma_start(rows[:, : S // 2], windows[h][:, : S // 2])
            nc.scalar.dma_start(rows[:, S // 2 :], windows[h][:, S // 2 :])
